import numpy as np
import ml_dtypes


def mxq(x, axis, fmt="e4m3"):
    dtype, down = {"e4m3": (ml_dtypes.float8_e4m3fn, 7), "e5m2": (ml_dtypes.float8_e5m2, 14)}[fmt]
    v = np.moveaxis(np.asarray(x, np.float32).astype(ml_dtypes.bfloat16).astype(np.float64), axis, -1)
    blocks = v.reshape(v.shape[:-1] + (-1, 32))
    amax = np.abs(blocks).max(-1, keepdims=True)
    byte = np.maximum(np.where(amax > 0, np.frexp(amax)[1] - 1 + 127, 0) - down, 1)
    scale = np.exp2(byte - 127.0)
    codes = (blocks / scale).astype(np.float32).astype(dtype).astype(np.float64)
    return np.moveaxis((codes * scale).reshape(v.shape), -1, axis)


WIDE = False


def mx_kscale(k):
    if not WIDE:
        return np.ones(k)
    levels = np.array([10, -10, 5, -5, 0])
    a = np.random.permutation(np.resize(levels, k // 512 * 4)).reshape(k // 512, 4)
    idx = np.arange(k)
    return np.exp2(a[idx // 512, idx % 128 // 32])


BF16 = ml_dtypes.bfloat16


def bf(x):
    return np.asarray(x, np.float32).astype(BF16)


def f64(x):
    return np.asarray(x).astype(np.float64)


E2M1 = np.array([0.0, 0.5, 1.0, 1.5, 2.0, 3.0, 4.0, 6.0, -0.0, -0.5, -1.0, -1.5, -2.0, -3.0, -4.0, -6.0])


def pack_weight(w, fmt):
    k, n = w.shape
    w = f64(bf(w)).reshape(k // 32, 32, n)
    amax = np.abs(w).max(1)
    if fmt == "e4m3":
        byte = np.frexp(amax)[1] - 1 + 127 - 7
    else:
        mant, ex = np.frexp(amax / 6.0)
        byte = np.where(mant > 0.5, ex, ex - 1) + 127
    byte = np.clip(np.where(amax > 0, byte, 1), 1, 254)
    scaled = (w * np.exp2(127.0 - byte)[:, None, :]).reshape(k, n).astype(np.float32)
    by_word = np.ascontiguousarray(scaled.reshape(k // 512, 128, 4, n).transpose(0, 1, 3, 2))
    if fmt == "e4m3":
        words = by_word.astype(ml_dtypes.float8_e4m3fn).view(np.uint8)
    else:
        c = by_word.astype(ml_dtypes.float4_e2m1fn).view(np.uint8) & 0xF
        words = c[..., 0::2] | (c[..., 1::2] << 4)
    return np.ascontiguousarray(words), np.ascontiguousarray(byte.astype(np.uint8).reshape(k // 512, 16, n))


def unpack_weight(words, scales, fmt):
    g, p, n, _ = words.shape
    if fmt == "e4m3":
        vals = np.ascontiguousarray(words).view(ml_dtypes.float8_e4m3fn).astype(np.float64)
    else:
        nib = np.empty((g, p, n, 4), np.uint8)
        nib[..., 0::2] = words & 0xF
        nib[..., 1::2] = words >> 4
        vals = E2M1[nib]
    vals = vals * np.repeat(np.exp2(scales.astype(np.float64) - 127.0), 8, axis=1)[..., None]
    return vals.transpose(0, 1, 3, 2).reshape(g * 512, n)


B, H = 512, 2048
DMN_FACTOR = 0.5
FMT = "e4m3"


def sigmoid(v):
    return 1.0 / (1.0 + np.exp(-v))


def setup_inputs():
    s = mx_kscale(H)
    x = bf(np.random.standard_normal((B, H)) * s)
    w = np.random.standard_normal((H, H)) / np.sqrt(H) / s[None, :]
    b = bf(np.random.standard_normal(H) * 0.1)
    plasticity_modulation = bf(np.random.uniform(0.0, 1.0, H) / s)
    cm = np.random.uniform(0.0, 1.0, (H, H)) * 6.0 * np.sqrt(H)
    W_words, W_scales = pack_weight(w.T, FMT)
    cm_words, cm_scales = pack_weight(cm.T, FMT)
    return {"x": x,
            "W_words": W_words,
            "W_scales": W_scales,
            "b": b,
            "plasticity_modulation": plasticity_modulation,
            "connectivity_mask_words": cm_words,
            "connectivity_mask_scales": cm_scales}


def reference(x, W_words, W_scales, b, plasticity_modulation, connectivity_mask_words, connectivity_mask_scales):
    x = f64(x)
    hn = x.shape[1]
    bdnf_effect = sigmoid((mxq(x, 1, "e4m3") @ unpack_weight(W_words, W_scales, FMT)) + f64(b))
    xs = x * f64(plasticity_modulation)
    g = mxq(xs, 1, "e4m3") @ unpack_weight(connectivity_mask_words, connectivity_mask_scales, FMT)
    fi = xs * g * (DMN_FACTOR / hn)
    return xs + bdnf_effect * fi

@@ -1,0 +1,209 @@
+from contextlib import ExitStack
+
+import concourse.mybir as mybir
+from concourse.masks import make_identity
+
+F32 = mybir.dt.float32
+BF16 = mybir.dt.bfloat16
+I32 = mybir.dt.int32
+U32 = mybir.dt.uint32
+U8 = mybir.dt.uint8
+FP8X4 = mybir.dt.float8_e4m3fn_x4
+ALU = mybir.AluOpType
+ACT = mybir.ActivationFunctionType
+
+P = 128
+PACK = 4
+K_PASS = P * PACK
+ROWS = 512
+H = 2048
+ROW_TILES = ROWS // P
+PASSES = H // K_PASS
+N_CHUNK = 512
+N_CHUNKS = H // N_CHUNK
+PLANE_STEP = 4
+DMN_SCALE = 0.5 / H
+
+FLOPS = 2 * 2 * ROWS * H * H
+
+
+def load_scale_planes(nc, planes, scales):
+    for quadrant in range(4):
+        nc.sync.dma_start(
+            out=planes[32 * quadrant : 32 * quadrant + 16, :].bitcast(I32),
+            in_=scales[:, 4 * quadrant : 4 * quadrant + 4, :].bitcast(I32),
+        )
+
+
+def load_weight_chunk(nc, words_sb, words, chunk):
+    by_partition = words.rearrange("g p n t -> p g (n t)")
+    nc.sync.dma_start(
+        out=words_sb[:, :, chunk * N_CHUNK : (chunk + 1) * N_CHUNK].bitcast(I32),
+        in_=by_partition[:, :, chunk * N_CHUNK * PACK : (chunk + 1) * N_CHUNK * PACK].bitcast(I32),
+    )
+
+
+def mx_sum(nc, acc, codes, code_scales, row_tile, words_sb, planes, chunk):
+    n_cols = slice(chunk * N_CHUNK, (chunk + 1) * N_CHUNK)
+    for g in range(PASSES):
+        rows = slice(g * P, (g + 1) * P)
+        nc.tensor.matmul_mx(
+            out=acc[:],
+            lhsT=codes[:, row_tile, rows].bitcast(FP8X4),
+            lhsT_scale=code_scales[:, row_tile, rows],
+            rhs=words_sb[:, g, n_cols].bitcast(FP8X4),
+            rhs_scale=planes[PLANE_STEP * g : P, n_cols],
+            start=(g == 0),
+            stop=(g == PASSES - 1),
+        )
+
+
+def tile_neuroplasticitymodule_kernel(
+    tc,
+    x,
+    W_words,
+    W_scales,
+    b,
+    plasticity_modulation,
+    connectivity_mask_words,
+    connectivity_mask_scales,
+    out,
+):
+    nc = tc.nc
+    with ExitStack() as ctx:
+        ctx.enter_context(tc.manual_schedule())
+        keep = ctx.enter_context(tc.tile_pool(name="keep", bufs=1))
+        work = ctx.enter_context(tc.tile_pool(name="work", bufs=ROW_TILES))
+        psum = ctx.enter_context(tc.psum_pool(name="psum", bufs=ROW_TILES))
+        bank_tags = ("z", "g")
+
+        w_planes = keep.tile([P, H], U8, name="w_planes", align_bytes=64)
+        cm_planes = keep.tile([P, H], U8, name="cm_planes", align_bytes=64)
+        vec_rows = keep.tile([P, 2 * H], BF16, name="vec_rows")
+        ones = keep.tile([P, P], BF16, name="ones")
+        warm = keep.tile([P, 1], F32, name="warm")
+        ident = keep.tile([P, P], F32, name="ident")
+        nc.vector.memset(vec_rows[:], 0.0)
+        nc.vector.memset(w_planes[:].bitcast(I32), 0)
+        nc.vector.memset(cm_planes[:].bitcast(I32), 0)
+        nc.vector.memset(ones[:], 1.0)
+        nc.vector.memset(warm[:], 0.0)
+        make_identity(nc, ident[:])
+
+        x_sb = keep.tile([P, ROW_TILES, H], BF16, name="x_sb")
+        for row_tile in range(ROW_TILES):
+            nc.sync.dma_start(out=x_sb[:, row_tile, :], in_=x[row_tile * P : (row_tile + 1) * P, :])
+        load_scale_planes(nc, w_planes, W_scales)
+        load_scale_planes(nc, cm_planes, connectivity_mask_scales)
+        w_words = keep.tile([P, PASSES, H], U32, name="w_words", align_bytes=64)
+        cm_words = keep.tile([P, PASSES, H], U32, name="cm_words", align_bytes=64)
+        for chunk in range(N_CHUNKS):
+            load_weight_chunk(nc, w_words, W_words, chunk)
+            load_weight_chunk(nc, cm_words, connectivity_mask_words, chunk)
+
+        pm_by_k = keep.tile([P, PASSES, PACK], BF16, name="pm_by_k")
+        nc.scalar.dma_start(
+            out=pm_by_k[:], in_=plasticity_modulation.rearrange("(g p t) -> p g t", g=PASSES, p=P, t=PACK)
+        )
+        nc.scalar.dma_start(out=vec_rows[0:1, 0:H], in_=b.rearrange("(o n) -> o n", o=1))
+        nc.scalar.dma_start(out=vec_rows[0:1, H : 2 * H], in_=plasticity_modulation.rearrange("(o n) -> o n", o=1))
+        nc.scalar.activation(out=warm[:], in_=warm[:], func=ACT.Sigmoid)
+
+        vec_all = keep.tile([P, 2 * H], BF16, name="vec_all")
+        b_all = vec_all[:, 0:H]
+        pm_all = vec_all[:, H : 2 * H]
+        for bank_index in range(2 * H // (2 * N_CHUNK)):
+            spread = psum.tile([P, 2 * N_CHUNK], BF16, name="spread", tag=bank_tags[bank_index % 2])
+            for half in range(2):
+                first = (2 * bank_index + half) * N_CHUNK
+                nc.tensor.matmul(
+                    out=spread[:, half * N_CHUNK : (half + 1) * N_CHUNK],
+                    lhsT=ones[:],
+                    rhs=vec_rows[:, first : first + N_CHUNK],
+                    start=True,
+                    stop=True,
+                )
+            nc.scalar.copy(out=vec_all[:, 2 * bank_index * N_CHUNK : 2 * (bank_index + 1) * N_CHUNK], in_=spread[:])
+
+        xs = keep.tile([P, ROW_TILES, H], F32, name="xs")
+        for chunk in range(N_CHUNKS):
+            n_cols = slice(chunk * N_CHUNK, (chunk + 1) * N_CHUNK)
+            for row_tile in range(ROW_TILES):
+                nc.gpsimd.tensor_tensor(
+                    out=xs[:, row_tile, n_cols], in0=x_sb[:, row_tile, n_cols], in1=pm_all[:, n_cols], op=ALU.mult
+                )
+
+        x_grouped = keep.tile([P, ROW_TILES, PASSES, P, PACK], BF16, name="x_grouped", align_bytes=64)
+        xs_grouped = keep.tile([P, ROW_TILES, PASSES, P, PACK], BF16, name="xs_grouped", align_bytes=64)
+        x_codes = keep.tile([P, ROW_TILES, PASSES * P], U32, name="x_codes", align_bytes=64)
+        xs_codes = keep.tile([P, ROW_TILES, PASSES * P], U32, name="xs_codes", align_bytes=64)
+        x_scales = keep.tile([P, ROW_TILES, PASSES * P], U8, name="x_scales", align_bytes=64)
+        xs_scales = keep.tile([P, ROW_TILES, PASSES * P], U8, name="xs_scales", align_bytes=64)
+
+        def transpose_x(row_tile):
+            x_pairs = x_sb[:, row_tile, :].bitcast(F32)
+            for bank_index in range(PASSES // 2):
+                flipped = psum.tile([P, 2, 2, P], F32, name="flipped", tag=bank_tags[bank_index % 2])
+                for g_in_bank in range(2):
+                    g = 2 * bank_index + g_in_bank
+                    for u in range(2):
+                        nc.tensor.transpose(
+                            flipped[:, g_in_bank, u, :],
+                            x_pairs[:, (K_PASS // 2) * g + u : (K_PASS // 2) * (g + 1) : 2],
+                            ident[:],
+                        )
+                nc.scalar.copy(
+                    out=x_grouped[:, row_tile, 2 * bank_index : 2 * bank_index + 2, :, :].bitcast(F32),
+                    in_=flipped[:].rearrange("p g u r -> p g r u"),
+                )
+
+        def quantise(grouped, codes, code_scales, row_tile):
+            nc.vector.quantize_mx(
+                out=codes[:, row_tile, :].bitcast(FP8X4),
+                scales=code_scales[:, row_tile, :],
+                in_=grouped[:, row_tile].rearrange("p g r t -> p (g r t)"),
+            )
+
+        def scale_by_modulation(row_tile):
+            nc.vector.tensor_tensor(
+                out=xs_grouped[:, row_tile],
+                in0=x_grouped[:, row_tile],
+                in1=pm_by_k[:].unsqueeze(2).to_broadcast([P, PASSES, P, PACK]),
+                op=ALU.mult,
+            )
+
+        for step in range(ROW_TILES + 2):
+            if step < ROW_TILES:
+                transpose_x(step)
+                quantise(x_grouped, x_codes, x_scales, step)
+            if 1 <= step <= ROW_TILES:
+                scale_by_modulation(step - 1)
+            if step >= 2:
+                quantise(xs_grouped, xs_codes, xs_scales, step - 2)
+
+        for chunk in range(N_CHUNKS):
+            n_cols = slice(chunk * N_CHUNK, (chunk + 1) * N_CHUNK)
+            gates = []
+            for row_tile in range(ROW_TILES):
+                z = psum.tile([P, N_CHUNK], F32, name="z", tag="z")
+                mx_sum(nc, z, x_codes, x_scales, row_tile, w_words, w_planes, chunk)
+                gate = work.tile([P, N_CHUNK], F32, name="gate")
+                nc.vector.tensor_tensor(out=gate[:], in0=z[:], in1=b_all[:, n_cols], op=ALU.add)
+                nc.scalar.activation(out=gate[:], in_=gate[:], func=ACT.Sigmoid)
+                gates.append(gate)
+            for row_tile in range(ROW_TILES):
+                g_sum = psum.tile([P, N_CHUNK], F32, name="g_sum", tag="g")
+                mx_sum(nc, g_sum, xs_codes, xs_scales, row_tile, cm_words, cm_planes, chunk)
+                gate = gates[row_tile]
+                nc.vector.scalar_tensor_tensor(
+                    out=gate[:], in0=g_sum[:], scalar=DMN_SCALE, in1=gate[:], op0=ALU.mult, op1=ALU.mult
+                )
+                nc.vector.scalar_tensor_tensor(
+                    out=xs[:, row_tile, n_cols],
+                    in0=gate[:],
+                    scalar=1.0,
+                    in1=xs[:, row_tile, n_cols],
+                    op0=ALU.add,
+                    op1=ALU.mult,
+                )
+                nc.sync.dma_start(out=out[row_tile * P : (row_tile + 1) * P, n_cols], in_=xs[:, row_tile, n_cols])

@@ -36,11 +36,11 @@ def load_scale_planes(nc, planes, scales):
 
 
 def load_weight_chunk(nc, words_sb, words, chunk):
-    by_partition = words.rearrange("g p n t -> p g (n t)")
-    nc.sync.dma_start(
-        out=words_sb[:, :, chunk * N_CHUNK : (chunk + 1) * N_CHUNK].bitcast(I32),
-        in_=by_partition[:, :, chunk * N_CHUNK * PACK : (chunk + 1) * N_CHUNK * PACK].bitcast(I32),
-    )
+    for g in range(PASSES):
+        nc.sync.dma_start(
+            out=words_sb[:, g, chunk * N_CHUNK : (chunk + 1) * N_CHUNK].bitcast(I32),
+            in_=words[g, :, chunk * N_CHUNK : (chunk + 1) * N_CHUNK, :].rearrange("p n t -> p (n t)").bitcast(I32),
+        )
 
 
 def mx_sum(nc, acc, codes, code_scales, row_tile, words_sb, planes, chunk):
@@ -73,7 +73,7 @@ def tile_neuroplasticitymodule_kernel(
     with ExitStack() as ctx:
         ctx.enter_context(tc.manual_schedule())
         keep = ctx.enter_context(tc.tile_pool(name="keep", bufs=1))
-        work = ctx.enter_context(tc.tile_pool(name="work", bufs=ROW_TILES))
+        work = ctx.enter_context(tc.tile_pool(name="work", bufs=2 * ROW_TILES))
         psum = ctx.enter_context(tc.psum_pool(name="psum", bufs=ROW_TILES))
         bank_tags = ("z", "g")
 
@@ -105,33 +105,9 @@ def tile_neuroplasticitymodule_kernel(
         nc.scalar.dma_start(
             out=pm_by_k[:], in_=plasticity_modulation.rearrange("(g p t) -> p g t", g=PASSES, p=P, t=PACK)
         )
-        nc.scalar.dma_start(out=vec_rows[0:1, 0:H], in_=b.rearrange("(o n) -> o n", o=1))
-        nc.scalar.dma_start(out=vec_rows[0:1, H : 2 * H], in_=plasticity_modulation.rearrange("(o n) -> o n", o=1))
+        nc.scalar.dma_start(out=vec_rows[0:1, 0:H], in_=plasticity_modulation.rearrange("(o n) -> o n", o=1))
+        nc.scalar.dma_start(out=vec_rows[0:1, H : 2 * H], in_=b.rearrange("(o n) -> o n", o=1))
         nc.scalar.activation(out=warm[:], in_=warm[:], func=ACT.Sigmoid)
-
-        vec_all = keep.tile([P, 2 * H], BF16, name="vec_all")
-        b_all = vec_all[:, 0:H]
-        pm_all = vec_all[:, H : 2 * H]
-        for bank_index in range(2 * H // (2 * N_CHUNK)):
-            spread = psum.tile([P, 2 * N_CHUNK], BF16, name="spread", tag=bank_tags[bank_index % 2])
-            for half in range(2):
-                first = (2 * bank_index + half) * N_CHUNK
-                nc.tensor.matmul(
-                    out=spread[:, half * N_CHUNK : (half + 1) * N_CHUNK],
-                    lhsT=ones[:],
-                    rhs=vec_rows[:, first : first + N_CHUNK],
-                    start=True,
-                    stop=True,
-                )
-            nc.scalar.copy(out=vec_all[:, 2 * bank_index * N_CHUNK : 2 * (bank_index + 1) * N_CHUNK], in_=spread[:])
-
-        xs = keep.tile([P, ROW_TILES, H], F32, name="xs")
-        for chunk in range(N_CHUNKS):
-            n_cols = slice(chunk * N_CHUNK, (chunk + 1) * N_CHUNK)
-            for row_tile in range(ROW_TILES):
-                nc.gpsimd.tensor_tensor(
-                    out=xs[:, row_tile, n_cols], in0=x_sb[:, row_tile, n_cols], in1=pm_all[:, n_cols], op=ALU.mult
-                )
 
         x_grouped = keep.tile([P, ROW_TILES, PASSES, P, PACK], BF16, name="x_grouped", align_bytes=64)
         xs_grouped = keep.tile([P, ROW_TILES, PASSES, P, PACK], BF16, name="xs_grouped", align_bytes=64)
@@ -181,9 +157,38 @@ def tile_neuroplasticitymodule_kernel(
             if step >= 2:
                 quantise(xs_grouped, xs_codes, xs_scales, step - 2)
 
+        vec_all = keep.tile([P, 2 * H], BF16, name="vec_all")
+        pm_all = vec_all[:, 0:H]
+        b_all = vec_all[:, H : 2 * H]
+        for bank_index in range(2 * H // (2 * N_CHUNK)):
+            spread = psum.tile([P, 2 * N_CHUNK], BF16, name="spread", tag=bank_tags[bank_index % 2])
+            for half in range(2):
+                first = (2 * bank_index + half) * N_CHUNK
+                nc.tensor.matmul(
+                    out=spread[:, half * N_CHUNK : (half + 1) * N_CHUNK],
+                    lhsT=ones[:],
+                    rhs=vec_rows[:, first : first + N_CHUNK],
+                    start=True,
+                    stop=True,
+                )
+            nc.scalar.copy(out=vec_all[:, 2 * bank_index * N_CHUNK : 2 * (bank_index + 1) * N_CHUNK], in_=spread[:])
+
+        xs = keep.tile([P, ROW_TILES, H], F32, name="xs")
+
+        def modulate(chunk):
+            n_cols = slice(chunk * N_CHUNK, (chunk + 1) * N_CHUNK)
+            for row_tile in range(ROW_TILES):
+                nc.gpsimd.tensor_tensor(
+                    out=xs[:, row_tile, n_cols], in0=x_sb[:, row_tile, n_cols], in1=pm_all[:, n_cols], op=ALU.mult
+                )
+
+        modulate(0)
+
         for chunk in range(N_CHUNKS):
             n_cols = slice(chunk * N_CHUNK, (chunk + 1) * N_CHUNK)
             gates = []
+            if chunk + 1 < N_CHUNKS:
+                modulate(chunk + 1)
             for row_tile in range(ROW_TILES):
                 z = psum.tile([P, N_CHUNK], F32, name="z", tag="z")
                 mx_sum(nc, z, x_codes, x_scales, row_tile, w_words, w_planes, chunk)
@@ -198,12 +203,18 @@ def tile_neuroplasticitymodule_kernel(
                 nc.vector.scalar_tensor_tensor(
                     out=gate[:], in0=g_sum[:], scalar=DMN_SCALE, in1=gate[:], op0=ALU.mult, op1=ALU.mult
                 )
-                nc.vector.scalar_tensor_tensor(
-                    out=xs[:, row_tile, n_cols],
-                    in0=gate[:],
-                    scalar=1.0,
-                    in1=xs[:, row_tile, n_cols],
-                    op0=ALU.add,
-                    op1=ALU.mult,
-                )
+                if row_tile % 2 == 0:
+                    nc.scalar.add(out=gate[:], in_=gate[:], add=1.0)
+                    nc.gpsimd.tensor_tensor(
+                        out=xs[:, row_tile, n_cols], in0=gate[:], in1=xs[:, row_tile, n_cols], op=ALU.mult
+                    )
+                else:
+                    nc.vector.scalar_tensor_tensor(
+                        out=xs[:, row_tile, n_cols],
+                        in0=gate[:],
+                        scalar=1.0,
+                        in1=xs[:, row_tile, n_cols],
+                        op0=ALU.add,
+                        op1=ALU.mult,
+                    )
                 nc.sync.dma_start(out=out[row_tile * P : (row_tile + 1) * P, n_cols], in_=xs[:, row_tile, n_cols])

@@ -23,6 +23,8 @@ N_CHUNK = 512
 N_CHUNKS = H // N_CHUNK
 PLANE_STEP = 4
 DMN_SCALE = 0.5 / H
+PSUM_BANKS = 8
+CHUNKS_TOGETHER = PSUM_BANKS // ROW_TILES
 
 FLOPS = 2 * 2 * ROWS * H * H
 
@@ -73,9 +75,8 @@ def tile_neuroplasticitymodule_kernel(
     with ExitStack() as ctx:
         ctx.enter_context(tc.manual_schedule())
         keep = ctx.enter_context(tc.tile_pool(name="keep", bufs=1))
-        work = ctx.enter_context(tc.tile_pool(name="work", bufs=2 * ROW_TILES))
-        psum = ctx.enter_context(tc.psum_pool(name="psum", bufs=ROW_TILES))
-        bank_tags = ("z", "g")
+        work = ctx.enter_context(tc.tile_pool(name="work", bufs=PSUM_BANKS))
+        psum = ctx.enter_context(tc.psum_pool(name="psum", bufs=PSUM_BANKS))
 
         w_planes = keep.tile([P, H], U8, name="w_planes", align_bytes=64)
         cm_planes = keep.tile([P, H], U8, name="cm_planes", align_bytes=64)
@@ -93,13 +94,18 @@ def tile_neuroplasticitymodule_kernel(
         x_sb = keep.tile([P, ROW_TILES, H], BF16, name="x_sb")
         for row_tile in range(ROW_TILES):
             nc.sync.dma_start(out=x_sb[:, row_tile, :], in_=x[row_tile * P : (row_tile + 1) * P, :])
-        load_scale_planes(nc, w_planes, W_scales)
-        load_scale_planes(nc, cm_planes, connectivity_mask_scales)
         w_words = keep.tile([P, PASSES, H], U32, name="w_words", align_bytes=64)
         cm_words = keep.tile([P, PASSES, H], U32, name="cm_words", align_bytes=64)
-        for chunk in range(N_CHUNKS):
-            load_weight_chunk(nc, w_words, W_words, chunk)
-            load_weight_chunk(nc, cm_words, connectivity_mask_words, chunk)
+        for first_chunk in range(0, N_CHUNKS, CHUNKS_TOGETHER):
+            chunks = range(first_chunk, first_chunk + CHUNKS_TOGETHER)
+            if first_chunk == 0:
+                load_scale_planes(nc, w_planes, W_scales)
+            for chunk in chunks:
+                load_weight_chunk(nc, w_words, W_words, chunk)
+            if first_chunk == 0:
+                load_scale_planes(nc, cm_planes, connectivity_mask_scales)
+            for chunk in chunks:
+                load_weight_chunk(nc, cm_words, connectivity_mask_words, chunk)
 
         pm_by_k = keep.tile([P, PASSES, PACK], BF16, name="pm_by_k")
         nc.scalar.dma_start(
@@ -119,7 +125,7 @@ def tile_neuroplasticitymodule_kernel(
         def transpose_x(row_tile):
             x_pairs = x_sb[:, row_tile, :].bitcast(F32)
             for bank_index in range(PASSES // 2):
-                flipped = psum.tile([P, 2, 2, P], F32, name="flipped", tag=bank_tags[bank_index % 2])
+                flipped = psum.tile([P, 2, 2, P], F32, name="flipped", tag="bank")
                 for g_in_bank in range(2):
                     g = 2 * bank_index + g_in_bank
                     for u in range(2):
@@ -161,7 +167,7 @@ def tile_neuroplasticitymodule_kernel(
         pm_all = vec_all[:, 0:H]
         b_all = vec_all[:, H : 2 * H]
         for bank_index in range(2 * H // (2 * N_CHUNK)):
-            spread = psum.tile([P, 2 * N_CHUNK], BF16, name="spread", tag=bank_tags[bank_index % 2])
+            spread = psum.tile([P, 2 * N_CHUNK], BF16, name="spread", tag="bank")
             for half in range(2):
                 first = (2 * bank_index + half) * N_CHUNK
                 nc.tensor.matmul(
@@ -182,39 +188,45 @@ def tile_neuroplasticitymodule_kernel(
                     out=xs[:, row_tile, n_cols], in0=x_sb[:, row_tile, n_cols], in1=pm_all[:, n_cols], op=ALU.mult
                 )
 
-        modulate(0)
+        for chunk in range(CHUNKS_TOGETHER):
+            modulate(chunk)
 
-        for chunk in range(N_CHUNKS):
-            n_cols = slice(chunk * N_CHUNK, (chunk + 1) * N_CHUNK)
-            gates = []
-            if chunk + 1 < N_CHUNKS:
-                modulate(chunk + 1)
-            for row_tile in range(ROW_TILES):
-                z = psum.tile([P, N_CHUNK], F32, name="z", tag="z")
-                mx_sum(nc, z, x_codes, x_scales, row_tile, w_words, w_planes, chunk)
-                gate = work.tile([P, N_CHUNK], F32, name="gate")
-                nc.vector.tensor_tensor(out=gate[:], in0=z[:], in1=b_all[:, n_cols], op=ALU.add)
-                nc.scalar.activation(out=gate[:], in_=gate[:], func=ACT.Sigmoid)
-                gates.append(gate)
-            for row_tile in range(ROW_TILES):
-                g_sum = psum.tile([P, N_CHUNK], F32, name="g_sum", tag="g")
-                mx_sum(nc, g_sum, xs_codes, xs_scales, row_tile, cm_words, cm_planes, chunk)
-                gate = gates[row_tile]
-                nc.vector.scalar_tensor_tensor(
-                    out=gate[:], in0=g_sum[:], scalar=DMN_SCALE, in1=gate[:], op0=ALU.mult, op1=ALU.mult
-                )
-                if row_tile % 2 == 0:
-                    nc.scalar.add(out=gate[:], in_=gate[:], add=1.0)
-                    nc.gpsimd.tensor_tensor(
-                        out=xs[:, row_tile, n_cols], in0=gate[:], in1=xs[:, row_tile, n_cols], op=ALU.mult
-                    )
-                else:
+        for first_chunk in range(0, N_CHUNKS, CHUNKS_TOGETHER):
+            chunks = range(first_chunk, first_chunk + CHUNKS_TOGETHER)
+            gates = {}
+            for chunk in chunks:
+                n_cols = slice(chunk * N_CHUNK, (chunk + 1) * N_CHUNK)
+                for row_tile in range(ROW_TILES):
+                    z = psum.tile([P, N_CHUNK], F32, name="z", tag="bank")
+                    mx_sum(nc, z, x_codes, x_scales, row_tile, w_words, w_planes, chunk)
+                    gate = work.tile([P, N_CHUNK], F32, name="gate")
+                    nc.vector.tensor_tensor(out=gate[:], in0=z[:], in1=b_all[:, n_cols], op=ALU.add)
+                    nc.scalar.activation(out=gate[:], in_=gate[:], func=ACT.Sigmoid)
+                    gates[(chunk, row_tile)] = gate
+            for chunk in chunks:
+                n_cols = slice(chunk * N_CHUNK, (chunk + 1) * N_CHUNK)
+                for row_tile in range(ROW_TILES):
+                    g_sum = psum.tile([P, N_CHUNK], F32, name="g_sum", tag="bank")
+                    mx_sum(nc, g_sum, xs_codes, xs_scales, row_tile, cm_words, cm_planes, chunk)
+                    gate = gates[(chunk, row_tile)]
                     nc.vector.scalar_tensor_tensor(
-                        out=xs[:, row_tile, n_cols],
-                        in0=gate[:],
-                        scalar=1.0,
-                        in1=xs[:, row_tile, n_cols],
-                        op0=ALU.add,
-                        op1=ALU.mult,
+                        out=gate[:], in0=g_sum[:], scalar=DMN_SCALE, in1=gate[:], op0=ALU.mult, op1=ALU.mult
                     )
-                nc.sync.dma_start(out=out[row_tile * P : (row_tile + 1) * P, n_cols], in_=xs[:, row_tile, n_cols])
+                    if row_tile % 2 == 0:
+                        nc.scalar.add(out=gate[:], in_=gate[:], add=1.0)
+                        nc.gpsimd.tensor_tensor(
+                            out=xs[:, row_tile, n_cols], in0=gate[:], in1=xs[:, row_tile, n_cols], op=ALU.mult
+                        )
+                    else:
+                        nc.vector.scalar_tensor_tensor(
+                            out=xs[:, row_tile, n_cols],
+                            in0=gate[:],
+                            scalar=1.0,
+                            in1=xs[:, row_tile, n_cols],
+                            op0=ALU.add,
+                            op1=ALU.mult,
+                        )
+                    nc.sync.dma_start(out=out[row_tile * P : (row_tile + 1) * P, n_cols], in_=xs[:, row_tile, n_cols])
+            for chunk in chunks:
+                if chunk + CHUNKS_TOGETHER < N_CHUNKS:
+                    modulate(chunk + CHUNKS_TOGETHER)

@@ -23,8 +23,7 @@ N_CHUNK = 512
 N_CHUNKS = H // N_CHUNK
 PLANE_STEP = 4
 DMN_SCALE = 0.5 / H
-PSUM_BANKS = 8
-CHUNKS_TOGETHER = PSUM_BANKS // ROW_TILES
+GPSIMD_ROW_TILES = 1
 
 FLOPS = 2 * 2 * ROWS * H * H
 
@@ -75,8 +74,9 @@ def tile_neuroplasticitymodule_kernel(
     with ExitStack() as ctx:
         ctx.enter_context(tc.manual_schedule())
         keep = ctx.enter_context(tc.tile_pool(name="keep", bufs=1))
-        work = ctx.enter_context(tc.tile_pool(name="work", bufs=PSUM_BANKS))
-        psum = ctx.enter_context(tc.psum_pool(name="psum", bufs=PSUM_BANKS))
+        work = ctx.enter_context(tc.tile_pool(name="work", bufs=2 * ROW_TILES))
+        psum = ctx.enter_context(tc.psum_pool(name="psum", bufs=ROW_TILES))
+        bank_tags = ("z", "g")
 
         w_planes = keep.tile([P, H], U8, name="w_planes", align_bytes=64)
         cm_planes = keep.tile([P, H], U8, name="cm_planes", align_bytes=64)
@@ -94,18 +94,13 @@ def tile_neuroplasticitymodule_kernel(
         x_sb = keep.tile([P, ROW_TILES, H], BF16, name="x_sb")
         for row_tile in range(ROW_TILES):
             nc.sync.dma_start(out=x_sb[:, row_tile, :], in_=x[row_tile * P : (row_tile + 1) * P, :])
+        load_scale_planes(nc, w_planes, W_scales)
+        load_scale_planes(nc, cm_planes, connectivity_mask_scales)
         w_words = keep.tile([P, PASSES, H], U32, name="w_words", align_bytes=64)
         cm_words = keep.tile([P, PASSES, H], U32, name="cm_words", align_bytes=64)
-        for first_chunk in range(0, N_CHUNKS, CHUNKS_TOGETHER):
-            chunks = range(first_chunk, first_chunk + CHUNKS_TOGETHER)
-            if first_chunk == 0:
-                load_scale_planes(nc, w_planes, W_scales)
-            for chunk in chunks:
-                load_weight_chunk(nc, w_words, W_words, chunk)
-            if first_chunk == 0:
-                load_scale_planes(nc, cm_planes, connectivity_mask_scales)
-            for chunk in chunks:
-                load_weight_chunk(nc, cm_words, connectivity_mask_words, chunk)
+        for chunk in range(N_CHUNKS):
+            load_weight_chunk(nc, w_words, W_words, chunk)
+            load_weight_chunk(nc, cm_words, connectivity_mask_words, chunk)
 
         pm_by_k = keep.tile([P, PASSES, PACK], BF16, name="pm_by_k")
         nc.scalar.dma_start(
@@ -125,7 +120,7 @@ def tile_neuroplasticitymodule_kernel(
         def transpose_x(row_tile):
             x_pairs = x_sb[:, row_tile, :].bitcast(F32)
             for bank_index in range(PASSES // 2):
-                flipped = psum.tile([P, 2, 2, P], F32, name="flipped", tag="bank")
+                flipped = psum.tile([P, 2, 2, P], F32, name="flipped", tag=bank_tags[bank_index % 2])
                 for g_in_bank in range(2):
                     g = 2 * bank_index + g_in_bank
                     for u in range(2):
@@ -167,7 +162,7 @@ def tile_neuroplasticitymodule_kernel(
         pm_all = vec_all[:, 0:H]
         b_all = vec_all[:, H : 2 * H]
         for bank_index in range(2 * H // (2 * N_CHUNK)):
-            spread = psum.tile([P, 2 * N_CHUNK], BF16, name="spread", tag="bank")
+            spread = psum.tile([P, 2 * N_CHUNK], BF16, name="spread", tag=bank_tags[bank_index % 2])
             for half in range(2):
                 first = (2 * bank_index + half) * N_CHUNK
                 nc.tensor.matmul(
@@ -188,45 +183,39 @@ def tile_neuroplasticitymodule_kernel(
                     out=xs[:, row_tile, n_cols], in0=x_sb[:, row_tile, n_cols], in1=pm_all[:, n_cols], op=ALU.mult
                 )
 
-        for chunk in range(CHUNKS_TOGETHER):
-            modulate(chunk)
+        modulate(0)
 
-        for first_chunk in range(0, N_CHUNKS, CHUNKS_TOGETHER):
-            chunks = range(first_chunk, first_chunk + CHUNKS_TOGETHER)
-            gates = {}
-            for chunk in chunks:
-                n_cols = slice(chunk * N_CHUNK, (chunk + 1) * N_CHUNK)
-                for row_tile in range(ROW_TILES):
-                    z = psum.tile([P, N_CHUNK], F32, name="z", tag="bank")
-                    mx_sum(nc, z, x_codes, x_scales, row_tile, w_words, w_planes, chunk)
-                    gate = work.tile([P, N_CHUNK], F32, name="gate")
-                    nc.vector.tensor_tensor(out=gate[:], in0=z[:], in1=b_all[:, n_cols], op=ALU.add)
-                    nc.scalar.activation(out=gate[:], in_=gate[:], func=ACT.Sigmoid)
-                    gates[(chunk, row_tile)] = gate
-            for chunk in chunks:
-                n_cols = slice(chunk * N_CHUNK, (chunk + 1) * N_CHUNK)
-                for row_tile in range(ROW_TILES):
-                    g_sum = psum.tile([P, N_CHUNK], F32, name="g_sum", tag="bank")
-                    mx_sum(nc, g_sum, xs_codes, xs_scales, row_tile, cm_words, cm_planes, chunk)
-                    gate = gates[(chunk, row_tile)]
-                    nc.vector.scalar_tensor_tensor(
-                        out=gate[:], in0=g_sum[:], scalar=DMN_SCALE, in1=gate[:], op0=ALU.mult, op1=ALU.mult
+        for chunk in range(N_CHUNKS):
+            n_cols = slice(chunk * N_CHUNK, (chunk + 1) * N_CHUNK)
+            gates = []
+            if chunk + 1 < N_CHUNKS:
+                modulate(chunk + 1)
+            for row_tile in range(ROW_TILES):
+                z = psum.tile([P, N_CHUNK], F32, name="z", tag="z")
+                mx_sum(nc, z, x_codes, x_scales, row_tile, w_words, w_planes, chunk)
+                gate = work.tile([P, N_CHUNK], F32, name="gate")
+                nc.vector.tensor_tensor(out=gate[:], in0=z[:], in1=b_all[:, n_cols], op=ALU.add)
+                nc.scalar.activation(out=gate[:], in_=gate[:], func=ACT.Sigmoid)
+                gates.append(gate)
+            for row_tile in range(ROW_TILES):
+                g_sum = psum.tile([P, N_CHUNK], F32, name="g_sum", tag="g")
+                mx_sum(nc, g_sum, xs_codes, xs_scales, row_tile, cm_words, cm_planes, chunk)
+                gate = gates[row_tile]
+                nc.vector.scalar_tensor_tensor(
+                    out=gate[:], in0=g_sum[:], scalar=DMN_SCALE, in1=gate[:], op0=ALU.mult, op1=ALU.mult
+                )
+                if row_tile < GPSIMD_ROW_TILES:
+                    nc.scalar.add(out=gate[:], in_=gate[:], add=1.0)
+                    nc.gpsimd.tensor_tensor(
+                        out=xs[:, row_tile, n_cols], in0=gate[:], in1=xs[:, row_tile, n_cols], op=ALU.mult
                     )
-                    if row_tile % 2 == 0:
-                        nc.scalar.add(out=gate[:], in_=gate[:], add=1.0)
-                        nc.gpsimd.tensor_tensor(
-                            out=xs[:, row_tile, n_cols], in0=gate[:], in1=xs[:, row_tile, n_cols], op=ALU.mult
-                        )
-                    else:
-                        nc.vector.scalar_tensor_tensor(
-                            out=xs[:, row_tile, n_cols],
-                            in0=gate[:],
-                            scalar=1.0,
-                            in1=xs[:, row_tile, n_cols],
-                            op0=ALU.add,
-                            op1=ALU.mult,
-                        )
-                    nc.sync.dma_start(out=out[row_tile * P : (row_tile + 1) * P, n_cols], in_=xs[:, row_tile, n_cols])
-            for chunk in chunks:
-                if chunk + CHUNKS_TOGETHER < N_CHUNKS:
-                    modulate(chunk + CHUNKS_TOGETHER)
+                else:
+                    nc.vector.scalar_tensor_tensor(
+                        out=xs[:, row_tile, n_cols],
+                        in0=gate[:],
+                        scalar=1.0,
+                        in1=xs[:, row_tile, n_cols],
+                        op0=ALU.add,
+                        op1=ALU.mult,
+                    )
+                nc.sync.dma_start(out=out[row_tile * P : (row_tile + 1) * P, n_cols], in_=xs[:, row_tile, n_cols])

@@ -23,7 +23,7 @@ N_CHUNK = 512
 N_CHUNKS = H // N_CHUNK
 PLANE_STEP = 4
 DMN_SCALE = 0.5 / H
-GPSIMD_ROW_TILES = 1
+GPSIMD_ROW_TILES = 2
 
 FLOPS = 2 * 2 * ROWS * H * H
 
@@ -174,48 +174,58 @@ def tile_neuroplasticitymodule_kernel(
                 )
             nc.scalar.copy(out=vec_all[:, 2 * bank_index * N_CHUNK : 2 * (bank_index + 1) * N_CHUNK], in_=spread[:])
 
-        xs = keep.tile([P, ROW_TILES, H], F32, name="xs")
+        xs_pool = ctx.enter_context(tc.tile_pool(name="xs_pool", bufs=2))
 
-        def modulate(chunk):
+        def modulate(chunk, row_tile):
             n_cols = slice(chunk * N_CHUNK, (chunk + 1) * N_CHUNK)
-            for row_tile in range(ROW_TILES):
-                nc.gpsimd.tensor_tensor(
-                    out=xs[:, row_tile, n_cols], in0=x_sb[:, row_tile, n_cols], in1=pm_all[:, n_cols], op=ALU.mult
-                )
+            xs = xs_pool.tile([P, N_CHUNK], F32, name="xs", tag="xs%d" % row_tile)
+            nc.gpsimd.tensor_tensor(out=xs[:], in0=x_sb[:, row_tile, n_cols], in1=pm_all[:, n_cols], op=ALU.mult)
+            return xs
 
-        modulate(0)
+        def store(chunk, row_tile, result):
+            nc.sync.dma_start(
+                out=out[row_tile * P : (row_tile + 1) * P, chunk * N_CHUNK : (chunk + 1) * N_CHUNK], in_=result[:]
+            )
 
+        def last_product(chunk, row_tile, gate, xs):
+            nc.vector.scalar_tensor_tensor(
+                out=xs[:], in0=gate[:], scalar=1.0, in1=xs[:], op0=ALU.add, op1=ALU.mult
+            )
+            store(chunk, row_tile, xs)
+
+        xs_tiles = {}
+        gates = {}
+        for row_tile in range(ROW_TILES):
+            xs_tiles[(0, row_tile)] = modulate(0, row_tile)
         for chunk in range(N_CHUNKS):
             n_cols = slice(chunk * N_CHUNK, (chunk + 1) * N_CHUNK)
-            gates = []
-            if chunk + 1 < N_CHUNKS:
-                modulate(chunk + 1)
+            last_chunk = chunk == N_CHUNKS - 1
             for row_tile in range(ROW_TILES):
                 z = psum.tile([P, N_CHUNK], F32, name="z", tag="z")
                 mx_sum(nc, z, x_codes, x_scales, row_tile, w_words, w_planes, chunk)
                 gate = work.tile([P, N_CHUNK], F32, name="gate")
                 nc.vector.tensor_tensor(out=gate[:], in0=z[:], in1=b_all[:, n_cols], op=ALU.add)
                 nc.scalar.activation(out=gate[:], in_=gate[:], func=ACT.Sigmoid)
-                gates.append(gate)
+                gates[(chunk, row_tile)] = gate
+                if chunk > 0:
+                    last_product(
+                        chunk - 1, row_tile, gates[(chunk - 1, row_tile)], xs_tiles[(chunk - 1, row_tile)]
+                    )
             for row_tile in range(ROW_TILES):
+                if not last_chunk:
+                    xs_tiles[(chunk + 1, row_tile)] = modulate(chunk + 1, row_tile)
                 g_sum = psum.tile([P, N_CHUNK], F32, name="g_sum", tag="g")
                 mx_sum(nc, g_sum, xs_codes, xs_scales, row_tile, cm_words, cm_planes, chunk)
-                gate = gates[row_tile]
+                gate = gates[(chunk, row_tile)]
                 nc.vector.scalar_tensor_tensor(
                     out=gate[:], in0=g_sum[:], scalar=DMN_SCALE, in1=gate[:], op0=ALU.mult, op1=ALU.mult
                 )
-                if row_tile < GPSIMD_ROW_TILES:
+                if last_chunk and row_tile < GPSIMD_ROW_TILES:
+                    xs = xs_tiles[(chunk, row_tile)]
                     nc.scalar.add(out=gate[:], in_=gate[:], add=1.0)
-                    nc.gpsimd.tensor_tensor(
-                        out=xs[:, row_tile, n_cols], in0=gate[:], in1=xs[:, row_tile, n_cols], op=ALU.mult
-                    )
-                else:
-                    nc.vector.scalar_tensor_tensor(
-                        out=xs[:, row_tile, n_cols],
-                        in0=gate[:],
-                        scalar=1.0,
-                        in1=xs[:, row_tile, n_cols],
-                        op0=ALU.add,
-                        op1=ALU.mult,
-                    )
-                nc.sync.dma_start(out=out[row_tile * P : (row_tile + 1) * P, n_cols], in_=xs[:, row_tile, n_cols])
+                    nc.gpsimd.tensor_tensor(out=xs[:], in0=gate[:], in1=xs[:], op=ALU.mult)
+                    store(chunk, row_tile, xs)
+        for row_tile in range(GPSIMD_ROW_TILES, ROW_TILES):
+            last_product(
+                N_CHUNKS - 1, row_tile, gates[(N_CHUNKS - 1, row_tile)], xs_tiles[(N_CHUNKS - 1, row_tile)]
+            )

@@ -23,7 +23,8 @@ N_CHUNK = 512
 N_CHUNKS = H // N_CHUNK
 PLANE_STEP = 4
 DMN_SCALE = 0.5 / H
-GPSIMD_ROW_TILES = 2
+VEC_RUN = H // P
+GPSIMD_ROW_TILES = 1
 
 FLOPS = 2 * 2 * ROWS * H * H
 
@@ -80,11 +81,12 @@ def tile_neuroplasticitymodule_kernel(
 
         w_planes = keep.tile([P, H], U8, name="w_planes", align_bytes=64)
         cm_planes = keep.tile([P, H], U8, name="cm_planes", align_bytes=64)
-        vec_rows = keep.tile([P, 2 * H], BF16, name="vec_rows")
+        pm_rows = keep.tile([P, H], BF16, name="pm_rows")
+        b_cols = keep.tile([P, VEC_RUN], BF16, name="b_cols")
         ones = keep.tile([P, P], BF16, name="ones")
         warm = keep.tile([P, 1], F32, name="warm")
         ident = keep.tile([P, P], F32, name="ident")
-        nc.vector.memset(vec_rows[:], 0.0)
+        nc.vector.memset(pm_rows[:], 0.0)
         nc.vector.memset(w_planes[:].bitcast(I32), 0)
         nc.vector.memset(cm_planes[:].bitcast(I32), 0)
         nc.vector.memset(ones[:], 1.0)
@@ -102,13 +104,30 @@ def tile_neuroplasticitymodule_kernel(
             load_weight_chunk(nc, w_words, W_words, chunk)
             load_weight_chunk(nc, cm_words, connectivity_mask_words, chunk)
 
+        nc.scalar.dma_start(out=b_cols[:], in_=b.rearrange("(p e) -> p e", e=VEC_RUN))
         pm_by_k = keep.tile([P, PASSES, PACK], BF16, name="pm_by_k")
         nc.scalar.dma_start(
             out=pm_by_k[:], in_=plasticity_modulation.rearrange("(g p t) -> p g t", g=PASSES, p=P, t=PACK)
         )
-        nc.scalar.dma_start(out=vec_rows[0:1, 0:H], in_=plasticity_modulation.rearrange("(o n) -> o n", o=1))
-        nc.scalar.dma_start(out=vec_rows[0:1, H : 2 * H], in_=b.rearrange("(o n) -> o n", o=1))
+        nc.scalar.dma_start(out=pm_rows[0:1, :], in_=plasticity_modulation.rearrange("(o n) -> o n", o=1))
         nc.scalar.activation(out=warm[:], in_=warm[:], func=ACT.Sigmoid)
+
+        vec_all = keep.tile([P, 2 * H], BF16, name="vec_all")
+        pm_all = vec_all[:, 0:H]
+        b_all = vec_all[:, H : 2 * H]
+        b_words = b_cols[:].bitcast(F32)
+        planes_in_bank = VEC_RUN // 4
+        for half in range(2):
+            spread = psum.tile([P, planes_in_bank, P], F32, name="spread", tag=bank_tags[half])
+            for c in range(planes_in_bank):
+                column = half * planes_in_bank + c
+                nc.tensor.transpose(spread[:, c, :], b_words[:, column : column + 1].to_broadcast([P, P]), ident[:])
+            nc.scalar.copy(
+                out=b_all.bitcast(F32).rearrange("j (p c) -> j p c", c=2 * planes_in_bank)[
+                    :, :, half * planes_in_bank : (half + 1) * planes_in_bank
+                ],
+                in_=spread[:].rearrange("j c p -> j p c"),
+            )
 
         x_grouped = keep.tile([P, ROW_TILES, PASSES, P, PACK], BF16, name="x_grouped", align_bytes=64)
         xs_grouped = keep.tile([P, ROW_TILES, PASSES, P, PACK], BF16, name="xs_grouped", align_bytes=64)
@@ -158,21 +177,18 @@ def tile_neuroplasticitymodule_kernel(
             if step >= 2:
                 quantise(xs_grouped, xs_codes, xs_scales, step - 2)
 
-        vec_all = keep.tile([P, 2 * H], BF16, name="vec_all")
-        pm_all = vec_all[:, 0:H]
-        b_all = vec_all[:, H : 2 * H]
-        for bank_index in range(2 * H // (2 * N_CHUNK)):
-            spread = psum.tile([P, 2 * N_CHUNK], BF16, name="spread", tag=bank_tags[bank_index % 2])
+        for bank_index in range(2):
+            spread = psum.tile([P, 2 * N_CHUNK], BF16, name="spread", tag=bank_tags[bank_index])
             for half in range(2):
                 first = (2 * bank_index + half) * N_CHUNK
                 nc.tensor.matmul(
                     out=spread[:, half * N_CHUNK : (half + 1) * N_CHUNK],
                     lhsT=ones[:],
-                    rhs=vec_rows[:, first : first + N_CHUNK],
+                    rhs=pm_rows[:, first : first + N_CHUNK],
                     start=True,
                     stop=True,
                 )
-            nc.scalar.copy(out=vec_all[:, 2 * bank_index * N_CHUNK : 2 * (bank_index + 1) * N_CHUNK], in_=spread[:])
+            nc.scalar.copy(out=pm_all[:, 2 * bank_index * N_CHUNK : 2 * (bank_index + 1) * N_CHUNK], in_=spread[:])
 
         xs_pool = ctx.enter_context(tc.tile_pool(name="xs_pool", bufs=2))
 
@@ -212,6 +228,8 @@ def tile_neuroplasticitymodule_kernel(
                         chunk - 1, row_tile, gates[(chunk - 1, row_tile)], xs_tiles[(chunk - 1, row_tile)]
                     )
             for row_tile in range(ROW_TILES):
+                if last_chunk and row_tile == ROW_TILES - 1:
+                    break
                 if not last_chunk:
                     xs_tiles[(chunk + 1, row_tile)] = modulate(chunk + 1, row_tile)
                 g_sum = psum.tile([P, N_CHUNK], F32, name="g_sum", tag="g")
@@ -225,7 +243,42 @@ def tile_neuroplasticitymodule_kernel(
                     nc.scalar.add(out=gate[:], in_=gate[:], add=1.0)
                     nc.gpsimd.tensor_tensor(out=xs[:], in0=gate[:], in1=xs[:], op=ALU.mult)
                     store(chunk, row_tile, xs)
-        for row_tile in range(GPSIMD_ROW_TILES, ROW_TILES):
-            last_product(
-                N_CHUNKS - 1, row_tile, gates[(N_CHUNKS - 1, row_tile)], xs_tiles[(N_CHUNKS - 1, row_tile)]
+                elif last_chunk and row_tile < ROW_TILES - 2:
+                    last_product(chunk, row_tile, gate, xs_tiles[(chunk, row_tile)])
+
+        chunk = N_CHUNKS - 1
+        row_tile = ROW_TILES - 1
+        gate = gates[(chunk, row_tile)]
+        xs = xs_tiles[(chunk, row_tile)]
+        half_width = N_CHUNK // 2
+
+        def half_sum(half):
+            acc = psum.tile([P, half_width], F32, name="half_sum", tag=bank_tags[half])
+            first = chunk * N_CHUNK + half * half_width
+            for g in range(PASSES):
+                nc.tensor.matmul_mx(
+                    out=acc[:],
+                    lhsT=xs_codes[:, row_tile, g * P : (g + 1) * P].bitcast(FP8X4),
+                    lhsT_scale=xs_scales[:, row_tile, g * P : (g + 1) * P],
+                    rhs=cm_words[:, g, first : first + half_width].bitcast(FP8X4),
+                    rhs_scale=cm_planes[PLANE_STEP * g : P, first : first + half_width],
+                    start=(g == 0),
+                    stop=(g == PASSES - 1),
+                )
+            cols = slice(half * half_width, (half + 1) * half_width)
+            nc.vector.scalar_tensor_tensor(
+                out=gate[:, cols], in0=acc[:], scalar=DMN_SCALE, in1=gate[:, cols], op0=ALU.mult, op1=ALU.mult
             )
+
+        def half_product(half):
+            cols = slice(half * half_width, (half + 1) * half_width)
+            nc.vector.scalar_tensor_tensor(
+                out=xs[:, cols], in0=gate[:, cols], scalar=1.0, in1=xs[:, cols], op0=ALU.add, op1=ALU.mult
+            )
+
+        half_sum(0)
+        last_product(chunk, row_tile - 1, gates[(chunk, row_tile - 1)], xs_tiles[(chunk, row_tile - 1)])
+        half_sum(1)
+        half_product(0)
+        half_product(1)
+        store(chunk, row_tile, xs)

@@ -45,19 +45,23 @@ def load_weight_chunk(nc, words_sb, words, chunk):
         )
 
 
-def mx_sum(nc, acc, codes, code_scales, row_tile, words_sb, planes, chunk):
+def mx_pass(nc, acc, codes, code_scales, row_tile, words_sb, planes, chunk, g):
     n_cols = slice(chunk * N_CHUNK, (chunk + 1) * N_CHUNK)
+    rows = slice(g * P, (g + 1) * P)
+    nc.tensor.matmul_mx(
+        out=acc[:],
+        lhsT=codes[:, row_tile, rows].bitcast(FP8X4),
+        lhsT_scale=code_scales[:, row_tile, rows],
+        rhs=words_sb[:, g, n_cols].bitcast(FP8X4),
+        rhs_scale=planes[PLANE_STEP * g : P, n_cols],
+        start=(g == 0),
+        stop=(g == PASSES - 1),
+    )
+
+
+def mx_sum(nc, acc, codes, code_scales, row_tile, words_sb, planes, chunk):
     for g in range(PASSES):
-        rows = slice(g * P, (g + 1) * P)
-        nc.tensor.matmul_mx(
-            out=acc[:],
-            lhsT=codes[:, row_tile, rows].bitcast(FP8X4),
-            lhsT_scale=code_scales[:, row_tile, rows],
-            rhs=words_sb[:, g, n_cols].bitcast(FP8X4),
-            rhs_scale=planes[PLANE_STEP * g : P, n_cols],
-            start=(g == 0),
-            stop=(g == PASSES - 1),
-        )
+        mx_pass(nc, acc, codes, code_scales, row_tile, words_sb, planes, chunk, g)
 
 
 def tile_neuroplasticitymodule_kernel(
@@ -96,12 +100,14 @@ def tile_neuroplasticitymodule_kernel(
         x_sb = keep.tile([P, ROW_TILES, H], BF16, name="x_sb")
         for row_tile in range(ROW_TILES):
             nc.sync.dma_start(out=x_sb[:, row_tile, :], in_=x[row_tile * P : (row_tile + 1) * P, :])
-        load_scale_planes(nc, w_planes, W_scales)
-        load_scale_planes(nc, cm_planes, connectivity_mask_scales)
         w_words = keep.tile([P, PASSES, H], U32, name="w_words", align_bytes=64)
         cm_words = keep.tile([P, PASSES, H], U32, name="cm_words", align_bytes=64)
         for chunk in range(N_CHUNKS):
+            if chunk == 0:
+                load_scale_planes(nc, w_planes, W_scales)
             load_weight_chunk(nc, w_words, W_words, chunk)
+            if chunk == 0:
+                load_scale_planes(nc, cm_planes, connectivity_mask_scales)
             load_weight_chunk(nc, cm_words, connectivity_mask_words, chunk)
 
         nc.scalar.dma_start(out=b_cols[:], in_=b.rearrange("(p e) -> p e", e=VEC_RUN))
@@ -216,9 +222,20 @@ def tile_neuroplasticitymodule_kernel(
         for chunk in range(N_CHUNKS):
             n_cols = slice(chunk * N_CHUNK, (chunk + 1) * N_CHUNK)
             last_chunk = chunk == N_CHUNKS - 1
+            first_sums = []
             for row_tile in range(ROW_TILES):
                 z = psum.tile([P, N_CHUNK], F32, name="z", tag="z")
-                mx_sum(nc, z, x_codes, x_scales, row_tile, w_words, w_planes, chunk)
+                first_sums.append(z)
+                if chunk == 0 and row_tile % 2 == 1:
+                    for g in range(PASSES):
+                        for one_of_pair in (row_tile - 1, row_tile):
+                            mx_pass(
+                                nc, first_sums[one_of_pair], x_codes, x_scales, one_of_pair, w_words, w_planes, chunk, g
+                            )
+            for row_tile in range(ROW_TILES):
+                z = first_sums[row_tile]
+                if chunk > 0:
+                    mx_sum(nc, z, x_codes, x_scales, row_tile, w_words, w_planes, chunk)
                 gate = work.tile([P, N_CHUNK], F32, name="gate")
                 nc.vector.tensor_tensor(out=gate[:], in0=z[:], in1=b_all[:, n_cols], op=ALU.add)
                 nc.scalar.activation(out=gate[:], in_=gate[:], func=ACT.Sigmoid)
@@ -232,8 +249,29 @@ def tile_neuroplasticitymodule_kernel(
                     break
                 if not last_chunk:
                     xs_tiles[(chunk + 1, row_tile)] = modulate(chunk + 1, row_tile)
-                g_sum = psum.tile([P, N_CHUNK], F32, name="g_sum", tag="g")
-                mx_sum(nc, g_sum, xs_codes, xs_scales, row_tile, cm_words, cm_planes, chunk)
+                if chunk == 0:
+                    if row_tile % 2 == 0:
+                        pair_sums = []
+                        for one_of_pair in range(2):
+                            g_sum = psum.tile([P, N_CHUNK], F32, name="g_sum", tag="g")
+                            pair_sums.append(g_sum)
+                        for g in range(PASSES):
+                            for one_of_pair in range(2):
+                                mx_pass(
+                                    nc,
+                                    pair_sums[one_of_pair],
+                                    xs_codes,
+                                    xs_scales,
+                                    row_tile + one_of_pair,
+                                    cm_words,
+                                    cm_planes,
+                                    chunk,
+                                    g,
+                                )
+                    g_sum = pair_sums[row_tile % 2]
+                else:
+                    g_sum = psum.tile([P, N_CHUNK], F32, name="g_sum", tag="g")
+                    mx_sum(nc, g_sum, xs_codes, xs_scales, row_tile, cm_words, cm_planes, chunk)
                 gate = gates[(chunk, row_tile)]
                 nc.vector.scalar_tensor_tensor(
                     out=gate[:], in0=g_sum[:], scalar=DMN_SCALE, in1=gate[:], op0=ALU.mult, op1=ALU.mult

from contextlib import ExitStack

import concourse.mybir as mybir
from concourse.masks import make_identity

F32 = mybir.dt.float32
BF16 = mybir.dt.bfloat16
I32 = mybir.dt.int32
U32 = mybir.dt.uint32
U8 = mybir.dt.uint8
FP8X4 = mybir.dt.float8_e4m3fn_x4
ALU = mybir.AluOpType
ACT = mybir.ActivationFunctionType

P = 128
PACK = 4
K_PASS = P * PACK
ROWS = 512
H = 2048
ROW_TILES = ROWS // P
PASSES = H // K_PASS
N_CHUNK = 512
N_CHUNKS = H // N_CHUNK
PLANE_STEP = 4
DMN_SCALE = 0.5 / H
VEC_RUN = H // P
GPSIMD_ROW_TILES = 1

FLOPS = 2 * 2 * ROWS * H * H


def load_scale_planes(nc, planes, scales):
    for quadrant in range(4):
        nc.sync.dma_start(
            out=planes[32 * quadrant : 32 * quadrant + 16, :].bitcast(I32),
            in_=scales[:, 4 * quadrant : 4 * quadrant + 4, :].bitcast(I32),
        )


def load_weight_chunk(nc, words_sb, words, chunk):
    for g in range(PASSES):
        nc.sync.dma_start(
            out=words_sb[:, g, chunk * N_CHUNK : (chunk + 1) * N_CHUNK].bitcast(I32),
            in_=words[g, :, chunk * N_CHUNK : (chunk + 1) * N_CHUNK, :].rearrange("p n t -> p (n t)").bitcast(I32),
        )


def mx_pass(nc, acc, codes, code_scales, row_tile, words_sb, planes, chunk, g):
    n_cols = slice(chunk * N_CHUNK, (chunk + 1) * N_CHUNK)
    rows = slice(g * P, (g + 1) * P)
    nc.tensor.matmul_mx(
        out=acc[:],
        lhsT=codes[:, row_tile, rows].bitcast(FP8X4),
        lhsT_scale=code_scales[:, row_tile, rows],
        rhs=words_sb[:, g, n_cols].bitcast(FP8X4),
        rhs_scale=planes[PLANE_STEP * g : P, n_cols],
        start=(g == 0),
        stop=(g == PASSES - 1),
    )


def mx_sum(nc, acc, codes, code_scales, row_tile, words_sb, planes, chunk):
    for g in range(PASSES):
        mx_pass(nc, acc, codes, code_scales, row_tile, words_sb, planes, chunk, g)


def tile_neuroplasticitymodule_kernel(
    tc,
    x,
    W_words,
    W_scales,
    b,
    plasticity_modulation,
    connectivity_mask_words,
    connectivity_mask_scales,
    out,
):
    nc = tc.nc
    with ExitStack() as ctx:
        ctx.enter_context(tc.manual_schedule())
        keep = ctx.enter_context(tc.tile_pool(name="keep", bufs=1))
        work = ctx.enter_context(tc.tile_pool(name="work", bufs=2 * ROW_TILES))
        psum = ctx.enter_context(tc.psum_pool(name="psum", bufs=ROW_TILES))
        bank_tags = ("z", "g")

        w_planes = keep.tile([P, H], U8, name="w_planes", align_bytes=64)
        cm_planes = keep.tile([P, H], U8, name="cm_planes", align_bytes=64)
        pm_rows = keep.tile([P, H], BF16, name="pm_rows")
        b_cols = keep.tile([P, VEC_RUN], BF16, name="b_cols")
        ones = keep.tile([P, P], BF16, name="ones")
        warm = keep.tile([P, 1], F32, name="warm")
        ident = keep.tile([P, P], F32, name="ident")
        nc.vector.memset(pm_rows[:], 0.0)
        nc.vector.memset(w_planes[:].bitcast(I32), 0)
        nc.vector.memset(cm_planes[:].bitcast(I32), 0)
        nc.vector.memset(ones[:], 1.0)
        nc.vector.memset(warm[:], 0.0)
        make_identity(nc, ident[:])

        x_sb = keep.tile([P, ROW_TILES, H], BF16, name="x_sb")
        for row_tile in range(ROW_TILES):
            nc.sync.dma_start(out=x_sb[:, row_tile, :], in_=x[row_tile * P : (row_tile + 1) * P, :])
        w_words = keep.tile([P, PASSES, H], U32, name="w_words", align_bytes=64)
        cm_words = keep.tile([P, PASSES, H], U32, name="cm_words", align_bytes=64)
        for chunk in range(N_CHUNKS):
            if chunk == 0:
                load_scale_planes(nc, w_planes, W_scales)
            load_weight_chunk(nc, w_words, W_words, chunk)
            if chunk == 0:
                load_scale_planes(nc, cm_planes, connectivity_mask_scales)
            load_weight_chunk(nc, cm_words, connectivity_mask_words, chunk)

        nc.scalar.dma_start(out=b_cols[:], in_=b.rearrange("(p e) -> p e", e=VEC_RUN))
        pm_by_k = keep.tile([P, PASSES, PACK], BF16, name="pm_by_k")
        nc.scalar.dma_start(
            out=pm_by_k[:], in_=plasticity_modulation.rearrange("(g p t) -> p g t", g=PASSES, p=P, t=PACK)
        )
        nc.scalar.dma_start(out=pm_rows[0:1, :], in_=plasticity_modulation.rearrange("(o n) -> o n", o=1))
        nc.scalar.activation(out=warm[:], in_=warm[:], func=ACT.Sigmoid)

        vec_all = keep.tile([P, 2 * H], BF16, name="vec_all")
        pm_all = vec_all[:, 0:H]
        b_all = vec_all[:, H : 2 * H]
        b_words = b_cols[:].bitcast(F32)
        planes_in_bank = VEC_RUN // 4
        for half in range(2):
            spread = psum.tile([P, planes_in_bank, P], F32, name="spread", tag=bank_tags[half])
            for c in range(planes_in_bank):
                column = half * planes_in_bank + c
                nc.tensor.transpose(spread[:, c, :], b_words[:, column : column + 1].to_broadcast([P, P]), ident[:])
            nc.scalar.copy(
                out=b_all.bitcast(F32).rearrange("j (p c) -> j p c", c=2 * planes_in_bank)[
                    :, :, half * planes_in_bank : (half + 1) * planes_in_bank
                ],
                in_=spread[:].rearrange("j c p -> j p c"),
            )

        x_grouped = keep.tile([P, ROW_TILES, PASSES, P, PACK], BF16, name="x_grouped", align_bytes=64)
        xs_grouped = keep.tile([P, ROW_TILES, PASSES, P, PACK], BF16, name="xs_grouped", align_bytes=64)
        x_codes = keep.tile([P, ROW_TILES, PASSES * P], U32, name="x_codes", align_bytes=64)
        xs_codes = keep.tile([P, ROW_TILES, PASSES * P], U32, name="xs_codes", align_bytes=64)
        x_scales = keep.tile([P, ROW_TILES, PASSES * P], U8, name="x_scales", align_bytes=64)
        xs_scales = keep.tile([P, ROW_TILES, PASSES * P], U8, name="xs_scales", align_bytes=64)

        def transpose_x(row_tile):
            x_pairs = x_sb[:, row_tile, :].bitcast(F32)
            for bank_index in range(PASSES // 2):
                flipped = psum.tile([P, 2, 2, P], F32, name="flipped", tag=bank_tags[bank_index % 2])
                for g_in_bank in range(2):
                    g = 2 * bank_index + g_in_bank
                    for u in range(2):
                        nc.tensor.transpose(
                            flipped[:, g_in_bank, u, :],
                            x_pairs[:, (K_PASS // 2) * g + u : (K_PASS // 2) * (g + 1) : 2],
                            ident[:],
                        )
                nc.scalar.copy(
                    out=x_grouped[:, row_tile, 2 * bank_index : 2 * bank_index + 2, :, :].bitcast(F32),
                    in_=flipped[:].rearrange("p g u r -> p g r u"),
                )

        def quantise(grouped, codes, code_scales, row_tile):
            nc.vector.quantize_mx(
                out=codes[:, row_tile, :].bitcast(FP8X4),
                scales=code_scales[:, row_tile, :],
                in_=grouped[:, row_tile].rearrange("p g r t -> p (g r t)"),
            )

        def scale_by_modulation(row_tile):
            nc.vector.tensor_tensor(
                out=xs_grouped[:, row_tile],
                in0=x_grouped[:, row_tile],
                in1=pm_by_k[:].unsqueeze(2).to_broadcast([P, PASSES, P, PACK]),
                op=ALU.mult,
            )

        for step in range(ROW_TILES + 2):
            if step < ROW_TILES:
                transpose_x(step)
                quantise(x_grouped, x_codes, x_scales, step)
            if 1 <= step <= ROW_TILES:
                scale_by_modulation(step - 1)
            if step >= 2:
                quantise(xs_grouped, xs_codes, xs_scales, step - 2)

        for bank_index in range(2):
            spread = psum.tile([P, 2 * N_CHUNK], BF16, name="spread", tag=bank_tags[bank_index])
            for half in range(2):
                first = (2 * bank_index + half) * N_CHUNK
                nc.tensor.matmul(
                    out=spread[:, half * N_CHUNK : (half + 1) * N_CHUNK],
                    lhsT=ones[:],
                    rhs=pm_rows[:, first : first + N_CHUNK],
                    start=True,
                    stop=True,
                )
            nc.scalar.copy(out=pm_all[:, 2 * bank_index * N_CHUNK : 2 * (bank_index + 1) * N_CHUNK], in_=spread[:])

        xs_pool = ctx.enter_context(tc.tile_pool(name="xs_pool", bufs=2))

        def modulate(chunk, row_tile):
            n_cols = slice(chunk * N_CHUNK, (chunk + 1) * N_CHUNK)
            xs = xs_pool.tile([P, N_CHUNK], F32, name="xs", tag="xs%d" % row_tile)
            nc.gpsimd.tensor_tensor(out=xs[:], in0=x_sb[:, row_tile, n_cols], in1=pm_all[:, n_cols], op=ALU.mult)
            return xs

        def store(chunk, row_tile, result):
            nc.sync.dma_start(
                out=out[row_tile * P : (row_tile + 1) * P, chunk * N_CHUNK : (chunk + 1) * N_CHUNK], in_=result[:]
            )

        def last_product(chunk, row_tile, gate, xs):
            nc.vector.scalar_tensor_tensor(
                out=xs[:], in0=gate[:], scalar=1.0, in1=xs[:], op0=ALU.add, op1=ALU.mult
            )
            store(chunk, row_tile, xs)

        xs_tiles = {}
        gates = {}
        for row_tile in range(ROW_TILES):
            xs_tiles[(0, row_tile)] = modulate(0, row_tile)
        for chunk in range(N_CHUNKS):
            n_cols = slice(chunk * N_CHUNK, (chunk + 1) * N_CHUNK)
            last_chunk = chunk == N_CHUNKS - 1
            first_sums = []
            for row_tile in range(ROW_TILES):
                z = psum.tile([P, N_CHUNK], F32, name="z", tag="z")
                first_sums.append(z)
                if chunk == 0 and row_tile % 2 == 1:
                    for g in range(PASSES):
                        for one_of_pair in (row_tile - 1, row_tile):
                            mx_pass(
                                nc, first_sums[one_of_pair], x_codes, x_scales, one_of_pair, w_words, w_planes, chunk, g
                            )
            for row_tile in range(ROW_TILES):
                z = first_sums[row_tile]
                if chunk > 0:
                    mx_sum(nc, z, x_codes, x_scales, row_tile, w_words, w_planes, chunk)
                gate = work.tile([P, N_CHUNK], F32, name="gate")
                nc.vector.tensor_tensor(out=gate[:], in0=z[:], in1=b_all[:, n_cols], op=ALU.add)
                nc.scalar.activation(out=gate[:], in_=gate[:], func=ACT.Sigmoid)
                gates[(chunk, row_tile)] = gate
                if chunk > 0:
                    last_product(
                        chunk - 1, row_tile, gates[(chunk - 1, row_tile)], xs_tiles[(chunk - 1, row_tile)]
                    )
            for row_tile in range(ROW_TILES):
                if last_chunk and row_tile == ROW_TILES - 1:
                    break
                if not last_chunk:
                    xs_tiles[(chunk + 1, row_tile)] = modulate(chunk + 1, row_tile)
                if chunk == 0:
                    if row_tile % 2 == 0:
                        pair_sums = []
                        for one_of_pair in range(2):
                            g_sum = psum.tile([P, N_CHUNK], F32, name="g_sum", tag="g")
                            pair_sums.append(g_sum)
                        for g in range(PASSES):
                            for one_of_pair in range(2):
                                mx_pass(
                                    nc,
                                    pair_sums[one_of_pair],
                                    xs_codes,
                                    xs_scales,
                                    row_tile + one_of_pair,
                                    cm_words,
                                    cm_planes,
                                    chunk,
                                    g,
                                )
                    g_sum = pair_sums[row_tile % 2]
                else:
                    g_sum = psum.tile([P, N_CHUNK], F32, name="g_sum", tag="g")
                    mx_sum(nc, g_sum, xs_codes, xs_scales, row_tile, cm_words, cm_planes, chunk)
                gate = gates[(chunk, row_tile)]
                nc.vector.scalar_tensor_tensor(
                    out=gate[:], in0=g_sum[:], scalar=DMN_SCALE, in1=gate[:], op0=ALU.mult, op1=ALU.mult
                )
                if last_chunk and row_tile < GPSIMD_ROW_TILES:
                    xs = xs_tiles[(chunk, row_tile)]
                    nc.scalar.add(out=gate[:], in_=gate[:], add=1.0)
                    nc.gpsimd.tensor_tensor(out=xs[:], in0=gate[:], in1=xs[:], op=ALU.mult)
                    store(chunk, row_tile, xs)
                elif last_chunk and row_tile < ROW_TILES - 2:
                    last_product(chunk, row_tile, gate, xs_tiles[(chunk, row_tile)])

        chunk = N_CHUNKS - 1
        row_tile = ROW_TILES - 1
        gate = gates[(chunk, row_tile)]
        xs = xs_tiles[(chunk, row_tile)]
        half_width = N_CHUNK // 2

        def half_sum(half):
            acc = psum.tile([P, half_width], F32, name="half_sum", tag=bank_tags[half])
            first = chunk * N_CHUNK + half * half_width
            for g in range(PASSES):
                nc.tensor.matmul_mx(
                    out=acc[:],
                    lhsT=xs_codes[:, row_tile, g * P : (g + 1) * P].bitcast(FP8X4),
                    lhsT_scale=xs_scales[:, row_tile, g * P : (g + 1) * P],
                    rhs=cm_words[:, g, first : first + half_width].bitcast(FP8X4),
                    rhs_scale=cm_planes[PLANE_STEP * g : P, first : first + half_width],
                    start=(g == 0),
                    stop=(g == PASSES - 1),
                )
            cols = slice(half * half_width, (half + 1) * half_width)
            nc.vector.scalar_tensor_tensor(
                out=gate[:, cols], in0=acc[:], scalar=DMN_SCALE, in1=gate[:, cols], op0=ALU.mult, op1=ALU.mult
            )

        def half_product(half):
            cols = slice(half * half_width, (half + 1) * half_width)
            nc.vector.scalar_tensor_tensor(
                out=xs[:, cols], in0=gate[:, cols], scalar=1.0, in1=xs[:, cols], op0=ALU.add, op1=ALU.mult
            )

        half_sum(0)
        last_product(chunk, row_tile - 1, gates[(chunk, row_tile - 1)], xs_tiles[(chunk, row_tile - 1)])
        half_sum(1)
        half_product(0)
        half_product(1)
        store(chunk, row_tile, xs)
